import numpy as np
import ml_dtypes


def mxq(x, axis, fmt="e4m3"):
    dtype, down = {"e4m3": (ml_dtypes.float8_e4m3fn, 7), "e5m2": (ml_dtypes.float8_e5m2, 14)}[fmt]
    v = np.moveaxis(np.asarray(x, np.float32).astype(ml_dtypes.bfloat16).astype(np.float64), axis, -1)
    blocks = v.reshape(v.shape[:-1] + (-1, 32))
    amax = np.abs(blocks).max(-1, keepdims=True)
    byte = np.maximum(np.where(amax > 0, np.frexp(amax)[1] - 1 + 127, 0) - down, 1)
    scale = np.exp2(byte - 127.0)
    codes = (blocks / scale).astype(np.float32).astype(dtype).astype(np.float64)
    return np.moveaxis((codes * scale).reshape(v.shape), -1, axis)


WIDE = False


def mx_kscale(k):
    if not WIDE:
        return np.ones(k)
    levels = np.array([10, -10, 5, -5, 0])
    a = np.random.permutation(np.resize(levels, k // 512 * 4)).reshape(k // 512, 4)
    idx = np.arange(k)
    return np.exp2(a[idx // 512, idx % 128 // 32])


BF16 = ml_dtypes.bfloat16


def bf(x):
    return np.asarray(x, np.float32).astype(BF16)


def f64(x):
    return np.asarray(x).astype(np.float64)


E2M1 = np.array([0.0, 0.5, 1.0, 1.5, 2.0, 3.0, 4.0, 6.0, -0.0, -0.5, -1.0, -1.5, -2.0, -3.0, -4.0, -6.0])


def pack_weight(w, fmt):
    k, n = w.shape
    w = f64(bf(w)).reshape(k // 32, 32, n)
    amax = np.abs(w).max(1)
    if fmt == "e4m3":
        byte = np.frexp(amax)[1] - 1 + 127 - 7
    else:
        mant, ex = np.frexp(amax / 6.0)
        byte = np.where(mant > 0.5, ex, ex - 1) + 127
    byte = np.clip(np.where(amax > 0, byte, 1), 1, 254)
    scaled = (w * np.exp2(127.0 - byte)[:, None, :]).reshape(k, n).astype(np.float32)
    by_word = np.ascontiguousarray(scaled.reshape(k // 512, 128, 4, n).transpose(0, 1, 3, 2))
    if fmt == "e4m3":
        words = by_word.astype(ml_dtypes.float8_e4m3fn).view(np.uint8)
    else:
        c = by_word.astype(ml_dtypes.float4_e2m1fn).view(np.uint8) & 0xF
        words = c[..., 0::2] | (c[..., 1::2] << 4)
    return np.ascontiguousarray(words), np.ascontiguousarray(byte.astype(np.uint8).reshape(k // 512, 16, n))


def unpack_weight(words, scales, fmt):
    g, p, n, _ = words.shape
    if fmt == "e4m3":
        vals = np.ascontiguousarray(words).view(ml_dtypes.float8_e4m3fn).astype(np.float64)
    else:
        nib = np.empty((g, p, n, 4), np.uint8)
        nib[..., 0::2] = words & 0xF
        nib[..., 1::2] = words >> 4
        vals = E2M1[nib]
    vals = vals * np.repeat(np.exp2(scales.astype(np.float64) - 127.0), 8, axis=1)[..., None]
    return vals.transpose(0, 1, 3, 2).reshape(g * 512, n)

def pack4(w):
    words, scales = pack_weight(w, "e2m1")
    return words.reshape(words.shape[0], 128, -1), scales


def unpack4(words, scales):
    return unpack_weight(words.reshape(words.shape[0], 128, -1, 2), scales, "e2m1")


E, D_NODE, D_EDGE, D_GLOB, LATENT, D_OUT = 16384, 128, 128, 128, 128, 128
D_IN = D_NODE + D_NODE + D_EDGE + D_GLOB


def setup_inputs():
    s = mx_kscale(D_IN)
    o1 = D_NODE
    o2 = o1 + D_NODE
    o3 = o2 + D_EDGE
    receiver = bf(np.random.standard_normal((E, D_NODE)) * s[:o1])
    sender = bf(np.random.standard_normal((E, D_NODE)) * s[o1:o2])
    edge_attr = bf(np.random.standard_normal((E, D_EDGE)) * s[o2:o3])
    global_attr = bf(np.random.standard_normal((1, D_GLOB)) * s[o3:])
    W1_words, W1_scales = pack4(np.random.standard_normal((D_IN, LATENT)) / np.sqrt(D_IN) / s[:, None])
    b1 = bf(np.random.standard_normal(LATENT) * 0.1)
    return {
        "receiver": receiver,
        "sender": sender,
        "edge_attr": edge_attr,
        "global_attr": global_attr,
        "W1_words": W1_words,
        "W1_scales": W1_scales,
        "b1": b1,
    }


def reference(receiver, sender, edge_attr, global_attr, W1_words, W1_scales, b1):
    e = edge_attr.shape[0]
    g = np.tile(f64(global_attr), (e // global_attr.shape[0], 1))
    x = np.concatenate([f64(receiver), f64(sender), f64(edge_attr), g], axis=1)
    return np.maximum((mxq(x, 1, "e4m3") @ unpack4(W1_words, W1_scales)) + f64(b1), 0.0)

@@ -1,0 +1,199 @@
+from contextlib import ExitStack
+
+import concourse.mybir as mybir
+from concourse.masks import make_identity
+
+BF16 = mybir.dt.bfloat16
+F32 = mybir.dt.float32
+I32 = mybir.dt.int32
+U32 = mybir.dt.uint32
+U8 = mybir.dt.uint8
+FP8X4 = mybir.dt.float8_e4m3fn_x4
+FP4X4 = mybir.dt.float4_e2m1fn_x4
+
+P = 128
+EDGES = 16384
+FEATURES = 128
+LATENT = 128
+PIECES = 4
+PACK = 4
+QUADS = 4
+QUAD = P // QUADS
+SLOTS = EDGES // P
+WORDS = FEATURES // 2
+WINDOW_COLS = QUADS * LATENT
+WINDOWS = 2
+ROUND_SLOTS = WINDOWS * QUADS
+ROUNDS = SLOTS // ROUND_SLOTS
+
+FLOPS = 2 * EDGES * PIECES * FEATURES * LATENT
+
+
+def tile_edgemodel_pa_t_kernel(
+    tc, receiver, sender, edge_attr, global_attr, W1_words, W1_scales, b1, out
+):
+    nc = tc.nc
+    inputs = (receiver, sender, edge_attr)
+    add = mybir.AluOpType.add
+    relu = mybir.ActivationFunctionType.Relu
+
+    with ExitStack() as ctx:
+        ctx.enter_context(tc.manual_schedule())
+        const = ctx.enter_context(tc.tile_pool(name="const", bufs=1))
+        x_pool = ctx.enter_context(tc.tile_pool(name="x", bufs=ROUNDS))
+        grouped_pool = ctx.enter_context(tc.tile_pool(name="grouped", bufs=4))
+        codes_pool = ctx.enter_context(tc.tile_pool(name="codes", bufs=9))
+        summed_pool = ctx.enter_context(tc.tile_pool(name="summed", bufs=3))
+        result_pool = ctx.enter_context(tc.tile_pool(name="result", bufs=ROUNDS))
+        flipped_psum = ctx.enter_context(tc.psum_pool(name="flipped", bufs=4))
+        acc_psum = ctx.enter_context(tc.psum_pool(name="acc", bufs=4))
+
+        w_words = const.tile([P, PIECES, 2 * WINDOW_COLS], U8, align_bytes=64)
+        w_scales = const.tile([P, PIECES, WINDOW_COLS], U8, align_bytes=64)
+        nc.vector.memset(w_words[:].rearrange("p s b -> p (s b)").bitcast(I32), 0)
+        nc.vector.memset(w_scales[:].rearrange("p s b -> p (s b)").bitcast(I32), 0)
+
+        identity = const.tile([P, P], F32)
+        make_identity(nc, identity[:])
+
+        x_tiles = []
+
+        def load_round(r):
+            tiles = []
+            for s in range(len(inputs)):
+                x_tile = x_pool.tile([P, ROUND_SLOTS, FEATURES], BF16, name="x%d" % s)
+                by_slot = inputs[s].rearrange("(p t) f -> p t f", t=SLOTS)
+                nc.sync.dma_start(
+                    out=x_tile[:], in_=by_slot[:, r * ROUND_SLOTS : (r + 1) * ROUND_SLOTS, :]
+                )
+                tiles.append(x_tile)
+            x_tiles.append(tiles)
+
+        load_round(0)
+        words_by_piece = W1_words[0].bitcast(I32).rearrange("(s i) b -> i s b", s=PIECES)
+        scales_by_piece = W1_scales[0].bitcast(I32).rearrange("(s r) b -> r s b", s=PIECES)
+        for q in range(QUADS):
+            nc.sync.dma_start(
+                out=w_words[
+                    q * QUAD : (q + 1) * QUAD, :, q * 2 * LATENT : (q + 1) * 2 * LATENT
+                ].bitcast(I32),
+                in_=words_by_piece,
+            )
+            nc.sync.dma_start(
+                out=w_scales[
+                    q * QUAD : q * QUAD + 4, :, q * LATENT : (q + 1) * LATENT
+                ].bitcast(I32),
+                in_=scales_by_piece,
+            )
+        for r in range(1, ROUNDS):
+            load_round(r)
+
+        g_rows = const.tile([P, PACK], BF16)
+        for q in range(QUADS):
+            nc.scalar.dma_start(
+                out=g_rows[q * QUAD : (q + 1) * QUAD, :],
+                in_=global_attr.rearrange("o (i t) -> (o i) t", t=PACK),
+            )
+        bias_rows = const.tile([P, LATENT], BF16)
+        nc.scalar.dma_start(out=bias_rows[:], in_=b1.partition_broadcast(P))
+
+        g_grouped = const.tile([P, P, PACK], BF16, align_bytes=64)
+        nc.vector.tensor_copy(
+            out=g_grouped[:], in_=g_rows[:].unsqueeze(1).to_broadcast([P, P, PACK])
+        )
+        g_codes = const.tile([P, P], U32, align_bytes=64)
+        g_plane = const.tile([P, P], U8, align_bytes=64)
+        nc.vector.quantize_mx(
+            out=g_codes[:].bitcast(FP8X4),
+            scales=g_plane[:],
+            in_=g_grouped[:].rearrange("p c t -> p (c t)"),
+        )
+        offset = const.tile([P, QUADS, LATENT], F32)
+
+        def global_and_bias():
+            g_acc = acc_psum.tile([P, WINDOW_COLS], F32, tag="acc")
+            nc.tensor.matmul_mx(
+                out=g_acc[:],
+                lhsT=g_codes[:].bitcast(FP8X4),
+                lhsT_scale=g_plane[:],
+                rhs=w_words[:, PIECES - 1, :].bitcast(FP4X4),
+                rhs_scale=w_scales[:, PIECES - 1, :],
+                start=True,
+                stop=True,
+            )
+            nc.vector.tensor_tensor(
+                out=offset[:],
+                in0=g_acc[:].rearrange("p (q n) -> p q n", q=QUADS),
+                in1=bias_rows[:].unsqueeze(1).to_broadcast([P, QUADS, LATENT]),
+                op=add,
+            )
+
+        quantised = []
+
+        def transpose_round(r):
+            operands = []
+            for s in range(len(inputs)):
+                words = x_tiles[r][s][:].rearrange("p t f -> p (t f)").bitcast(F32)
+                flipped = flipped_psum.tile([P, WINDOWS, 2, P], F32)
+                for w in range(WINDOWS):
+                    first = w * QUADS * WORDS
+                    for u in range(2):
+                        nc.tensor.transpose(
+                            flipped[:, w, u, :],
+                            words[:, first + u : first + QUADS * WORDS : 2],
+                            identity[:],
+                        )
+                grouped = grouped_pool.tile([P, WINDOWS * P * PACK], BF16, align_bytes=64)
+                nc.scalar.copy(
+                    out=grouped[:].bitcast(F32).rearrange(
+                        "k (w e u) -> k w e u", w=WINDOWS, u=2
+                    ),
+                    in_=flipped[:].rearrange("k w u e -> k w e u"),
+                )
+                codes = codes_pool.tile([P, WINDOWS * P], U32, align_bytes=64)
+                plane = codes_pool.tile([P, WINDOWS * P], U8, align_bytes=64)
+                nc.vector.quantize_mx(
+                    out=codes[:].bitcast(FP8X4), scales=plane[:], in_=grouped[:]
+                )
+                operands.append((codes, plane))
+            quantised.append(operands)
+
+        out_by_slot = out.rearrange("(p t) n -> p t n", t=SLOTS)
+
+        def multiply_round(r):
+            result = result_pool.tile([P, WINDOWS, WINDOW_COLS], F32)
+            for w in range(WINDOWS):
+                edges = slice(w * P, (w + 1) * P)
+                acc = acc_psum.tile([P, WINDOW_COLS], F32)
+                for s in range(len(inputs)):
+                    codes, plane = quantised[r][s]
+                    nc.tensor.matmul_mx(
+                        out=acc[:],
+                        lhsT=codes[:, edges].bitcast(FP8X4),
+                        lhsT_scale=plane[:, edges],
+                        rhs=w_words[:, s, :].bitcast(FP4X4),
+                        rhs_scale=w_scales[:, s, :],
+                        start=(s == 0),
+                        stop=(s == len(inputs) - 1),
+                    )
+                summed = summed_pool.tile([P, WINDOW_COLS], F32)
+                nc.vector.tensor_tensor(
+                    out=summed[:],
+                    in0=acc[:],
+                    in1=offset[:].rearrange("p q n -> p (q n)"),
+                    op=add,
+                )
+                nc.scalar.activation(out=result[:, w, :], in_=summed[:], func=relu)
+            nc.sync.dma_start(
+                out=out_by_slot[:, r * ROUND_SLOTS : (r + 1) * ROUND_SLOTS, :],
+                in_=result[:].rearrange("p w (q n) -> p (w q) n", n=LATENT),
+            )
+
+        transpose_round(0)
+        transpose_round(1)
+        global_and_bias()
+        multiply_round(0)
+        for r in range(2, ROUNDS):
+            transpose_round(r)
+            multiply_round(r - 1)
+        multiply_round(ROUNDS - 1)

@@ -20,7 +20,6 @@ PACK = 4
 QUADS = 4
 QUAD = P // QUADS
 SLOTS = EDGES // P
-WORDS = FEATURES // 2
 WINDOW_COLS = QUADS * LATENT
 WINDOWS = 2
 ROUND_SLOTS = WINDOWS * QUADS
@@ -41,9 +40,9 @@ def tile_edgemodel_pa_t_kernel(
         ctx.enter_context(tc.manual_schedule())
         const = ctx.enter_context(tc.tile_pool(name="const", bufs=1))
         x_pool = ctx.enter_context(tc.tile_pool(name="x", bufs=ROUNDS))
+        sorted_pool = ctx.enter_context(tc.tile_pool(name="sorted", bufs=3))
         grouped_pool = ctx.enter_context(tc.tile_pool(name="grouped", bufs=4))
         codes_pool = ctx.enter_context(tc.tile_pool(name="codes", bufs=9))
-        summed_pool = ctx.enter_context(tc.tile_pool(name="summed", bufs=3))
         result_pool = ctx.enter_context(tc.tile_pool(name="result", bufs=ROUNDS))
         flipped_psum = ctx.enter_context(tc.psum_pool(name="flipped", bufs=4))
         acc_psum = ctx.enter_context(tc.psum_pool(name="acc", bufs=4))
@@ -97,20 +96,20 @@ def tile_edgemodel_pa_t_kernel(
         bias_rows = const.tile([P, LATENT], BF16)
         nc.scalar.dma_start(out=bias_rows[:], in_=b1.partition_broadcast(P))
 
-        g_grouped = const.tile([P, P, PACK], BF16, align_bytes=64)
-        nc.vector.tensor_copy(
-            out=g_grouped[:], in_=g_rows[:].unsqueeze(1).to_broadcast([P, P, PACK])
-        )
-        g_codes = const.tile([P, P], U32, align_bytes=64)
-        g_plane = const.tile([P, P], U8, align_bytes=64)
-        nc.vector.quantize_mx(
-            out=g_codes[:].bitcast(FP8X4),
-            scales=g_plane[:],
-            in_=g_grouped[:].rearrange("p c t -> p (c t)"),
-        )
         offset = const.tile([P, QUADS, LATENT], F32)
 
         def global_and_bias():
+            g_grouped = const.tile([P, P, PACK], BF16, align_bytes=64)
+            nc.vector.tensor_copy(
+                out=g_grouped[:], in_=g_rows[:].unsqueeze(1).to_broadcast([P, P, PACK])
+            )
+            g_codes = const.tile([P, P], U32, align_bytes=64)
+            g_plane = const.tile([P, P], U8, align_bytes=64)
+            nc.vector.quantize_mx(
+                out=g_codes[:].bitcast(FP8X4),
+                scales=g_plane[:],
+                in_=g_grouped[:].rearrange("p c t -> p (c t)"),
+            )
             g_acc = acc_psum.tile([P, WINDOW_COLS], F32, tag="acc")
             nc.tensor.matmul_mx(
                 out=g_acc[:],
@@ -128,20 +127,30 @@ def tile_edgemodel_pa_t_kernel(
                 op=add,
             )
 
+        sorted_tiles = []
+
+        def sort_round(r):
+            tiles = []
+            for s in range(len(inputs)):
+                words = x_tiles[r][s][:].rearrange("p t f -> p (t f)").bitcast(F32)
+                in_runs = sorted_pool.tile([P, WINDOWS, 2, P], F32, name="sorted%d" % s)
+                nc.vector.tensor_copy(
+                    out=in_runs[:],
+                    in_=words.rearrange("p (w c u) -> p w u c", w=WINDOWS, u=2),
+                )
+                tiles.append(in_runs)
+            sorted_tiles.append(tiles)
+
         quantised = []
 
         def transpose_round(r):
             operands = []
             for s in range(len(inputs)):
-                words = x_tiles[r][s][:].rearrange("p t f -> p (t f)").bitcast(F32)
                 flipped = flipped_psum.tile([P, WINDOWS, 2, P], F32)
                 for w in range(WINDOWS):
-                    first = w * QUADS * WORDS
                     for u in range(2):
                         nc.tensor.transpose(
-                            flipped[:, w, u, :],
-                            words[:, first + u : first + QUADS * WORDS : 2],
-                            identity[:],
+                            flipped[:, w, u, :], sorted_tiles[r][s][:, w, u, :], identity[:]
                         )
                 grouped = grouped_pool.tile([P, WINDOWS * P * PACK], BF16, align_bytes=64)
                 nc.scalar.copy(
@@ -160,8 +169,11 @@ def tile_edgemodel_pa_t_kernel(
 
         out_by_slot = out.rearrange("(p t) n -> p t n", t=SLOTS)
 
+        results = []
+
         def multiply_round(r):
             result = result_pool.tile([P, WINDOWS, WINDOW_COLS], F32)
+            results.append(result)
             for w in range(WINDOWS):
                 edges = slice(w * P, (w + 1) * P)
                 acc = acc_psum.tile([P, WINDOW_COLS], F32)
@@ -176,24 +188,34 @@ def tile_edgemodel_pa_t_kernel(
                         start=(s == 0),
                         stop=(s == len(inputs) - 1),
                     )
-                summed = summed_pool.tile([P, WINDOW_COLS], F32)
                 nc.vector.tensor_tensor(
-                    out=summed[:],
+                    out=result[:, w, :],
                     in0=acc[:],
                     in1=offset[:].rearrange("p q n -> p (q n)"),
                     op=add,
                 )
-                nc.scalar.activation(out=result[:, w, :], in_=summed[:], func=relu)
+
+        def finish_round(r):
+            result = results[r]
+            nc.scalar.activation(out=result[:], in_=result[:], func=relu)
             nc.sync.dma_start(
                 out=out_by_slot[:, r * ROUND_SLOTS : (r + 1) * ROUND_SLOTS, :],
                 in_=result[:].rearrange("p w (q n) -> p (w q) n", n=LATENT),
             )
 
+        sort_round(0)
+        sort_round(1)
         transpose_round(0)
+        sort_round(2)
         transpose_round(1)
         global_and_bias()
         multiply_round(0)
         for r in range(2, ROUNDS):
+            if r + 1 < ROUNDS:
+                sort_round(r + 1)
             transpose_round(r)
             multiply_round(r - 1)
+            finish_round(r - 2)
         multiply_round(ROUNDS - 1)
+        finish_round(ROUNDS - 2)
+        finish_round(ROUNDS - 1)

@@ -41,7 +41,7 @@ def tile_edgemodel_pa_t_kernel(
         const = ctx.enter_context(tc.tile_pool(name="const", bufs=1))
         x_pool = ctx.enter_context(tc.tile_pool(name="x", bufs=ROUNDS))
         sorted_pool = ctx.enter_context(tc.tile_pool(name="sorted", bufs=3))
-        grouped_pool = ctx.enter_context(tc.tile_pool(name="grouped", bufs=4))
+        grouped_pool = ctx.enter_context(tc.tile_pool(name="grouped", bufs=7))
         codes_pool = ctx.enter_context(tc.tile_pool(name="codes", bufs=9))
         result_pool = ctx.enter_context(tc.tile_pool(name="result", bufs=ROUNDS))
         flipped_psum = ctx.enter_context(tc.psum_pool(name="flipped", bufs=4))
@@ -98,7 +98,9 @@ def tile_edgemodel_pa_t_kernel(
 
         offset = const.tile([P, QUADS, LATENT], F32)
 
-        def global_and_bias():
+        g_acc = acc_psum.tile([P, WINDOW_COLS], F32, tag="acc")
+
+        def multiply_global():
             g_grouped = const.tile([P, P, PACK], BF16, align_bytes=64)
             nc.vector.tensor_copy(
                 out=g_grouped[:], in_=g_rows[:].unsqueeze(1).to_broadcast([P, P, PACK])
@@ -110,7 +112,6 @@ def tile_edgemodel_pa_t_kernel(
                 scales=g_plane[:],
                 in_=g_grouped[:].rearrange("p c t -> p (c t)"),
             )
-            g_acc = acc_psum.tile([P, WINDOW_COLS], F32, tag="acc")
             nc.tensor.matmul_mx(
                 out=g_acc[:],
                 lhsT=g_codes[:].bitcast(FP8X4),
@@ -120,6 +121,8 @@ def tile_edgemodel_pa_t_kernel(
                 start=True,
                 stop=True,
             )
+
+        def make_offset():
             nc.vector.tensor_tensor(
                 out=offset[:],
                 in0=g_acc[:].rearrange("p (q n) -> p q n", q=QUADS),
@@ -141,10 +144,10 @@ def tile_edgemodel_pa_t_kernel(
                 tiles.append(in_runs)
             sorted_tiles.append(tiles)
 
-        quantised = []
+        grouped_tiles = []
 
         def transpose_round(r):
-            operands = []
+            tiles = []
             for s in range(len(inputs)):
                 flipped = flipped_psum.tile([P, WINDOWS, 2, P], F32)
                 for w in range(WINDOWS):
@@ -159,21 +162,28 @@ def tile_edgemodel_pa_t_kernel(
                     ),
                     in_=flipped[:].rearrange("k w u e -> k w e u"),
                 )
+                tiles.append(grouped)
+            grouped_tiles.append(tiles)
+
+        quantised = []
+
+        def quantise_round(r):
+            operands = []
+            for s in range(len(inputs)):
                 codes = codes_pool.tile([P, WINDOWS * P], U32, align_bytes=64)
                 plane = codes_pool.tile([P, WINDOWS * P], U8, align_bytes=64)
                 nc.vector.quantize_mx(
-                    out=codes[:].bitcast(FP8X4), scales=plane[:], in_=grouped[:]
+                    out=codes[:].bitcast(FP8X4), scales=plane[:], in_=grouped_tiles[r][s][:]
                 )
                 operands.append((codes, plane))
             quantised.append(operands)
 
         out_by_slot = out.rearrange("(p t) n -> p t n", t=SLOTS)
 
-        results = []
+        sums = []
 
         def multiply_round(r):
-            result = result_pool.tile([P, WINDOWS, WINDOW_COLS], F32)
-            results.append(result)
+            banks = []
             for w in range(WINDOWS):
                 edges = slice(w * P, (w + 1) * P)
                 acc = acc_psum.tile([P, WINDOW_COLS], F32)
@@ -188,9 +198,18 @@ def tile_edgemodel_pa_t_kernel(
                         start=(s == 0),
                         stop=(s == len(inputs) - 1),
                     )
+                banks.append(acc)
+            sums.append(banks)
+
+        results = []
+
+        def add_round(r):
+            result = result_pool.tile([P, WINDOWS, WINDOW_COLS], F32)
+            results.append(result)
+            for w in range(WINDOWS):
                 nc.vector.tensor_tensor(
                     out=result[:, w, :],
-                    in0=acc[:],
+                    in0=sums[r][w][:],
                     in1=offset[:].rearrange("p q n -> p (q n)"),
                     op=add,
                 )
@@ -203,19 +222,26 @@ def tile_edgemodel_pa_t_kernel(
                 in_=result[:].rearrange("p w (q n) -> p (w q) n", n=LATENT),
             )
 
+        def if_round(stage, r):
+            if 0 <= r < ROUNDS:
+                stage(r)
+
         sort_round(0)
         sort_round(1)
         transpose_round(0)
         sort_round(2)
         transpose_round(1)
-        global_and_bias()
+        quantise_round(0)
+        multiply_global()
+        sort_round(3)
+        transpose_round(2)
+        quantise_round(1)
         multiply_round(0)
-        for r in range(2, ROUNDS):
-            if r + 1 < ROUNDS:
-                sort_round(r + 1)
-            transpose_round(r)
-            multiply_round(r - 1)
-            finish_round(r - 2)
-        multiply_round(ROUNDS - 1)
-        finish_round(ROUNDS - 2)
-        finish_round(ROUNDS - 1)
+        make_offset()
+        for step in range(3, ROUNDS + 4):
+            if_round(finish_round, step - 4)
+            if_round(sort_round, step + 1)
+            if_round(transpose_round, step)
+            if_round(quantise_round, step - 1)
+            if_round(multiply_round, step - 2)
+            if_round(add_round, step - 3)

@@ -20,6 +20,7 @@ PACK = 4
 QUADS = 4
 QUAD = P // QUADS
 SLOTS = EDGES // P
+WORDS = FEATURES // 2
 WINDOW_COLS = QUADS * LATENT
 WINDOWS = 2
 ROUND_SLOTS = WINDOWS * QUADS
@@ -40,8 +41,7 @@ def tile_edgemodel_pa_t_kernel(
         ctx.enter_context(tc.manual_schedule())
         const = ctx.enter_context(tc.tile_pool(name="const", bufs=1))
         x_pool = ctx.enter_context(tc.tile_pool(name="x", bufs=ROUNDS))
-        sorted_pool = ctx.enter_context(tc.tile_pool(name="sorted", bufs=3))
-        grouped_pool = ctx.enter_context(tc.tile_pool(name="grouped", bufs=7))
+        grouped_pool = ctx.enter_context(tc.tile_pool(name="grouped", bufs=4))
         codes_pool = ctx.enter_context(tc.tile_pool(name="codes", bufs=9))
         result_pool = ctx.enter_context(tc.tile_pool(name="result", bufs=ROUNDS))
         flipped_psum = ctx.enter_context(tc.psum_pool(name="flipped", bufs=4))
@@ -96,22 +96,21 @@ def tile_edgemodel_pa_t_kernel(
         bias_rows = const.tile([P, LATENT], BF16)
         nc.scalar.dma_start(out=bias_rows[:], in_=b1.partition_broadcast(P))
 
+        g_grouped = const.tile([P, P, PACK], BF16, align_bytes=64)
+        nc.vector.tensor_copy(
+            out=g_grouped[:], in_=g_rows[:].unsqueeze(1).to_broadcast([P, P, PACK])
+        )
+        g_codes = const.tile([P, P], U32, align_bytes=64)
+        g_plane = const.tile([P, P], U8, align_bytes=64)
+        nc.vector.quantize_mx(
+            out=g_codes[:].bitcast(FP8X4),
+            scales=g_plane[:],
+            in_=g_grouped[:].rearrange("p c t -> p (c t)"),
+        )
         offset = const.tile([P, QUADS, LATENT], F32)
 
-        g_acc = acc_psum.tile([P, WINDOW_COLS], F32, tag="acc")
-
-        def multiply_global():
-            g_grouped = const.tile([P, P, PACK], BF16, align_bytes=64)
-            nc.vector.tensor_copy(
-                out=g_grouped[:], in_=g_rows[:].unsqueeze(1).to_broadcast([P, P, PACK])
-            )
-            g_codes = const.tile([P, P], U32, align_bytes=64)
-            g_plane = const.tile([P, P], U8, align_bytes=64)
-            nc.vector.quantize_mx(
-                out=g_codes[:].bitcast(FP8X4),
-                scales=g_plane[:],
-                in_=g_grouped[:].rearrange("p c t -> p (c t)"),
-            )
+        def global_and_bias():
+            g_acc = acc_psum.tile([P, WINDOW_COLS], F32, tag="acc")
             nc.tensor.matmul_mx(
                 out=g_acc[:],
                 lhsT=g_codes[:].bitcast(FP8X4),
@@ -121,8 +120,6 @@ def tile_edgemodel_pa_t_kernel(
                 start=True,
                 stop=True,
             )
-
-        def make_offset():
             nc.vector.tensor_tensor(
                 out=offset[:],
                 in0=g_acc[:].rearrange("p (q n) -> p q n", q=QUADS),
@@ -130,30 +127,20 @@ def tile_edgemodel_pa_t_kernel(
                 op=add,
             )
 
-        sorted_tiles = []
-
-        def sort_round(r):
-            tiles = []
-            for s in range(len(inputs)):
-                words = x_tiles[r][s][:].rearrange("p t f -> p (t f)").bitcast(F32)
-                in_runs = sorted_pool.tile([P, WINDOWS, 2, P], F32, name="sorted%d" % s)
-                nc.vector.tensor_copy(
-                    out=in_runs[:],
-                    in_=words.rearrange("p (w c u) -> p w u c", w=WINDOWS, u=2),
-                )
-                tiles.append(in_runs)
-            sorted_tiles.append(tiles)
-
-        grouped_tiles = []
+        quantised = []
 
         def transpose_round(r):
-            tiles = []
+            operands = []
             for s in range(len(inputs)):
+                words = x_tiles[r][s][:].rearrange("p t f -> p (t f)").bitcast(F32)
                 flipped = flipped_psum.tile([P, WINDOWS, 2, P], F32)
                 for w in range(WINDOWS):
+                    first = w * QUADS * WORDS
                     for u in range(2):
                         nc.tensor.transpose(
-                            flipped[:, w, u, :], sorted_tiles[r][s][:, w, u, :], identity[:]
+                            flipped[:, w, u, :],
+                            words[:, first + u : first + QUADS * WORDS : 2],
+                            identity[:],
                         )
                 grouped = grouped_pool.tile([P, WINDOWS * P * PACK], BF16, align_bytes=64)
                 nc.scalar.copy(
@@ -162,28 +149,21 @@ def tile_edgemodel_pa_t_kernel(
                     ),
                     in_=flipped[:].rearrange("k w u e -> k w e u"),
                 )
-                tiles.append(grouped)
-            grouped_tiles.append(tiles)
-
-        quantised = []
-
-        def quantise_round(r):
-            operands = []
-            for s in range(len(inputs)):
                 codes = codes_pool.tile([P, WINDOWS * P], U32, align_bytes=64)
                 plane = codes_pool.tile([P, WINDOWS * P], U8, align_bytes=64)
                 nc.vector.quantize_mx(
-                    out=codes[:].bitcast(FP8X4), scales=plane[:], in_=grouped_tiles[r][s][:]
+                    out=codes[:].bitcast(FP8X4), scales=plane[:], in_=grouped[:]
                 )
                 operands.append((codes, plane))
             quantised.append(operands)
 
         out_by_slot = out.rearrange("(p t) n -> p t n", t=SLOTS)
 
-        sums = []
+        results = []
 
         def multiply_round(r):
-            banks = []
+            result = result_pool.tile([P, WINDOWS, WINDOW_COLS], F32)
+            results.append(result)
             for w in range(WINDOWS):
                 edges = slice(w * P, (w + 1) * P)
                 acc = acc_psum.tile([P, WINDOW_COLS], F32)
@@ -198,18 +178,9 @@ def tile_edgemodel_pa_t_kernel(
                         start=(s == 0),
                         stop=(s == len(inputs) - 1),
                     )
-                banks.append(acc)
-            sums.append(banks)
-
-        results = []
-
-        def add_round(r):
-            result = result_pool.tile([P, WINDOWS, WINDOW_COLS], F32)
-            results.append(result)
-            for w in range(WINDOWS):
                 nc.vector.tensor_tensor(
                     out=result[:, w, :],
-                    in0=sums[r][w][:],
+                    in0=acc[:],
                     in1=offset[:].rearrange("p q n -> p (q n)"),
                     op=add,
                 )
@@ -222,26 +193,14 @@ def tile_edgemodel_pa_t_kernel(
                 in_=result[:].rearrange("p w (q n) -> p (w q) n", n=LATENT),
             )
 
-        def if_round(stage, r):
-            if 0 <= r < ROUNDS:
-                stage(r)
-
-        sort_round(0)
-        sort_round(1)
         transpose_round(0)
-        sort_round(2)
         transpose_round(1)
-        quantise_round(0)
-        multiply_global()
-        sort_round(3)
-        transpose_round(2)
-        quantise_round(1)
+        global_and_bias()
         multiply_round(0)
-        make_offset()
-        for step in range(3, ROUNDS + 4):
-            if_round(finish_round, step - 4)
-            if_round(sort_round, step + 1)
-            if_round(transpose_round, step)
-            if_round(quantise_round, step - 1)
-            if_round(multiply_round, step - 2)
-            if_round(add_round, step - 3)
+        for r in range(2, ROUNDS):
+            transpose_round(r)
+            multiply_round(r - 1)
+            finish_round(r - 2)
+        multiply_round(ROUNDS - 1)
+        finish_round(ROUNDS - 2)
+        finish_round(ROUNDS - 1)

@@ -16,17 +16,39 @@ EDGES = 16384
 FEATURES = 128
 LATENT = 128
 PIECES = 4
+BIG = 3
 PACK = 4
 QUADS = 4
 QUAD = P // QUADS
 SLOTS = EDGES // P
 WORDS = FEATURES // 2
-WINDOW_COLS = QUADS * LATENT
-WINDOWS = 2
-ROUND_SLOTS = WINDOWS * QUADS
+HALF = WORDS // 2
+ROUND_SLOTS = 8
 ROUNDS = SLOTS // ROUND_SLOTS
+ROUND_WORDS = ROUND_SLOTS * BIG * HALF
+OPERANDS = ROUND_WORDS // P
+UNIT_SLOTS = 4
+UNITS = ROUND_SLOTS // UNIT_SLOTS
+VARIANTS = 7
 
 FLOPS = 2 * EDGES * PIECES * FEATURES * LATENT
+
+PASSES = (
+    (0, 0, 0, True, True),
+    (0, 1, 1, True, False),
+    (1, 1, 2, False, True),
+    (1, 2, 3, True, False),
+    (2, 2, 4, False, True),
+    (2, 3, 5, True, True),
+)
+WEIGHT_LOADS = (
+    (0, 0, 2, 0, 4),
+    (3, 1, 2, 0, 3),
+    (1, 0, 2, 1, 2),
+    (1, 5, 1, 0, 1),
+    (2, 3, 2, 0, 2),
+    (2, 0, 1, 2, 1),
+)
 
 
 def tile_edgemodel_pa_t_kernel(
@@ -41,14 +63,15 @@ def tile_edgemodel_pa_t_kernel(
         ctx.enter_context(tc.manual_schedule())
         const = ctx.enter_context(tc.tile_pool(name="const", bufs=1))
         x_pool = ctx.enter_context(tc.tile_pool(name="x", bufs=ROUNDS))
+        sorted_pool = ctx.enter_context(tc.tile_pool(name="sorted", bufs=4))
         grouped_pool = ctx.enter_context(tc.tile_pool(name="grouped", bufs=4))
         codes_pool = ctx.enter_context(tc.tile_pool(name="codes", bufs=9))
-        result_pool = ctx.enter_context(tc.tile_pool(name="result", bufs=ROUNDS))
+        result_pool = ctx.enter_context(tc.tile_pool(name="result", bufs=6))
         flipped_psum = ctx.enter_context(tc.psum_pool(name="flipped", bufs=4))
         acc_psum = ctx.enter_context(tc.psum_pool(name="acc", bufs=4))
 
-        w_words = const.tile([P, PIECES, 2 * WINDOW_COLS], U8, align_bytes=64)
-        w_scales = const.tile([P, PIECES, WINDOW_COLS], U8, align_bytes=64)
+        w_words = const.tile([P, VARIANTS, 2 * LATENT], U8, align_bytes=64)
+        w_scales = const.tile([P, VARIANTS, LATENT], U8, align_bytes=64)
         nc.vector.memset(w_words[:].rearrange("p s b -> p (s b)").bitcast(I32), 0)
         nc.vector.memset(w_scales[:].rearrange("p s b -> p (s b)").bitcast(I32), 0)
 
@@ -58,31 +81,27 @@ def tile_edgemodel_pa_t_kernel(
         x_tiles = []
 
         def load_round(r):
-            tiles = []
-            for s in range(len(inputs)):
-                x_tile = x_pool.tile([P, ROUND_SLOTS, FEATURES], BF16, name="x%d" % s)
+            x_tile = x_pool.tile([P, BIG, ROUND_SLOTS, FEATURES], BF16, name="x")
+            for s in range(BIG):
                 by_slot = inputs[s].rearrange("(p t) f -> p t f", t=SLOTS)
                 nc.sync.dma_start(
-                    out=x_tile[:], in_=by_slot[:, r * ROUND_SLOTS : (r + 1) * ROUND_SLOTS, :]
+                    out=x_tile[:, s, :, :],
+                    in_=by_slot[:, r * ROUND_SLOTS : (r + 1) * ROUND_SLOTS, :],
                 )
-                tiles.append(x_tile)
-            x_tiles.append(tiles)
+            x_tiles.append(x_tile)
 
         load_round(0)
         words_by_piece = W1_words[0].bitcast(I32).rearrange("(s i) b -> i s b", s=PIECES)
         scales_by_piece = W1_scales[0].bitcast(I32).rearrange("(s r) b -> r s b", s=PIECES)
-        for q in range(QUADS):
+        for q, v0, vstep, s0, count in WEIGHT_LOADS:
+            variants = slice(v0, v0 + vstep * (count - 1) + 1, vstep)
             nc.sync.dma_start(
-                out=w_words[
-                    q * QUAD : (q + 1) * QUAD, :, q * 2 * LATENT : (q + 1) * 2 * LATENT
-                ].bitcast(I32),
-                in_=words_by_piece,
+                out=w_words[q * QUAD : (q + 1) * QUAD, variants, :].bitcast(I32),
+                in_=words_by_piece[:, s0 : s0 + count, :],
             )
             nc.sync.dma_start(
-                out=w_scales[
-                    q * QUAD : q * QUAD + 4, :, q * LATENT : (q + 1) * LATENT
-                ].bitcast(I32),
-                in_=scales_by_piece,
+                out=w_scales[q * QUAD : q * QUAD + 4, variants, :].bitcast(I32),
+                in_=scales_by_piece[:, s0 : s0 + count, :],
             )
         for r in range(1, ROUNDS):
             load_round(r)
@@ -97,60 +116,79 @@ def tile_edgemodel_pa_t_kernel(
         nc.scalar.dma_start(out=bias_rows[:], in_=b1.partition_broadcast(P))
 
         g_grouped = const.tile([P, P, PACK], BF16, align_bytes=64)
-        nc.vector.tensor_copy(
-            out=g_grouped[:], in_=g_rows[:].unsqueeze(1).to_broadcast([P, P, PACK])
-        )
         g_codes = const.tile([P, P], U32, align_bytes=64)
         g_plane = const.tile([P, P], U8, align_bytes=64)
-        nc.vector.quantize_mx(
-            out=g_codes[:].bitcast(FP8X4),
-            scales=g_plane[:],
-            in_=g_grouped[:].rearrange("p c t -> p (c t)"),
-        )
-        offset = const.tile([P, QUADS, LATENT], F32)
+        offset = const.tile([P, UNIT_SLOTS, LATENT], F32)
+
+        def quantise_global():
+            nc.vector.tensor_copy(
+                out=g_grouped[:], in_=g_rows[:].unsqueeze(1).to_broadcast([P, P, PACK])
+            )
+            nc.vector.quantize_mx(
+                out=g_codes[:].bitcast(FP8X4),
+                scales=g_plane[:],
+                in_=g_grouped[:].rearrange("p c t -> p (c t)"),
+            )
 
         def global_and_bias():
-            g_acc = acc_psum.tile([P, WINDOW_COLS], F32, tag="acc")
+            g_acc = acc_psum.tile([P, UNIT_SLOTS * LATENT], F32, tag="acc")
             nc.tensor.matmul_mx(
-                out=g_acc[:],
+                out=g_acc[:, 0:LATENT],
                 lhsT=g_codes[:].bitcast(FP8X4),
                 lhsT_scale=g_plane[:],
-                rhs=w_words[:, PIECES - 1, :].bitcast(FP4X4),
-                rhs_scale=w_scales[:, PIECES - 1, :],
+                rhs=w_words[:, VARIANTS - 1, :].bitcast(FP4X4),
+                rhs_scale=w_scales[:, VARIANTS - 1, :],
                 start=True,
                 stop=True,
             )
             nc.vector.tensor_tensor(
                 out=offset[:],
-                in0=g_acc[:].rearrange("p (q n) -> p q n", q=QUADS),
-                in1=bias_rows[:].unsqueeze(1).to_broadcast([P, QUADS, LATENT]),
+                in0=g_acc[:, 0:LATENT].unsqueeze(1).to_broadcast([P, UNIT_SLOTS, LATENT]),
+                in1=bias_rows[:].unsqueeze(1).to_broadcast([P, UNIT_SLOTS, LATENT]),
                 op=add,
             )
+
+        sorted_tiles = []
+
+        def sort_round(r):
+            words = (
+                x_tiles[r][:]
+                .rearrange("p s t f -> p (s t f)")
+                .bitcast(F32)
+                .rearrange("p (s t i u) -> p u t s i", s=BIG, t=ROUND_SLOTS, u=2)
+            )
+            in_order = sorted_pool.tile([P, 2, ROUND_WORDS], F32)
+            for u in range(2):
+                nc.vector.tensor_copy(
+                    out=in_order[:, u, :].rearrange(
+                        "p (t s i) -> p t s i", t=ROUND_SLOTS, s=BIG
+                    ),
+                    in_=words[:, u],
+                )
+            sorted_tiles.append(in_order)
 
         quantised = []
 
         def transpose_round(r):
             operands = []
-            for s in range(len(inputs)):
-                words = x_tiles[r][s][:].rearrange("p t f -> p (t f)").bitcast(F32)
-                flipped = flipped_psum.tile([P, WINDOWS, 2, P], F32)
-                for w in range(WINDOWS):
-                    first = w * QUADS * WORDS
+            in_order = sorted_tiles[r]
+            for b in range(OPERANDS // 2):
+                flipped = flipped_psum.tile([P, 2, 2, P], F32)
+                for w in range(2):
+                    j = 2 * b + w
                     for u in range(2):
                         nc.tensor.transpose(
                             flipped[:, w, u, :],
-                            words[:, first + u : first + QUADS * WORDS : 2],
+                            in_order[:, u, j * P : (j + 1) * P],
                             identity[:],
                         )
-                grouped = grouped_pool.tile([P, WINDOWS * P * PACK], BF16, align_bytes=64)
+                grouped = grouped_pool.tile([P, 2 * P * PACK], BF16, align_bytes=64)
                 nc.scalar.copy(
-                    out=grouped[:].bitcast(F32).rearrange(
-                        "k (w e u) -> k w e u", w=WINDOWS, u=2
-                    ),
+                    out=grouped[:].bitcast(F32).rearrange("k (w e u) -> k w e u", w=2, u=2),
                     in_=flipped[:].rearrange("k w u e -> k w e u"),
                 )
-                codes = codes_pool.tile([P, WINDOWS * P], U32, align_bytes=64)
-                plane = codes_pool.tile([P, WINDOWS * P], U8, align_bytes=64)
+                codes = codes_pool.tile([P, 2 * P], U32, align_bytes=64)
+                plane = codes_pool.tile([P, 2 * P], U8, align_bytes=64)
                 nc.vector.quantize_mx(
                     out=codes[:].bitcast(FP8X4), scales=plane[:], in_=grouped[:]
                 )
@@ -158,28 +196,28 @@ def tile_edgemodel_pa_t_kernel(
             quantised.append(operands)
 
         out_by_slot = out.rearrange("(p t) n -> p t n", t=SLOTS)
-
         results = []
 
         def multiply_round(r):
-            result = result_pool.tile([P, WINDOWS, WINDOW_COLS], F32)
+            result = result_pool.tile([P, UNITS, UNIT_SLOTS * LATENT], F32)
             results.append(result)
-            for w in range(WINDOWS):
-                edges = slice(w * P, (w + 1) * P)
-                acc = acc_psum.tile([P, WINDOW_COLS], F32)
-                for s in range(len(inputs)):
-                    codes, plane = quantised[r][s]
+            for h in range(UNITS):
+                acc = acc_psum.tile([P, UNIT_SLOTS * LATENT], F32)
+                for operand, slot, variant, start, stop in PASSES:
+                    j = 3 * h + operand
+                    codes, plane = quantised[r][j // 2]
+                    edges = slice((j % 2) * P, (j % 2 + 1) * P)
                     nc.tensor.matmul_mx(
-                        out=acc[:],
+                        out=acc[:, slot * LATENT : (slot + 1) * LATENT],
                         lhsT=codes[:, edges].bitcast(FP8X4),
                         lhsT_scale=plane[:, edges],
-                        rhs=w_words[:, s, :].bitcast(FP4X4),
-                        rhs_scale=w_scales[:, s, :],
-                        start=(s == 0),
-                        stop=(s == len(inputs) - 1),
+                        rhs=w_words[:, variant, :].bitcast(FP4X4),
+                        rhs_scale=w_scales[:, variant, :],
+                        start=start,
+                        stop=stop,
                     )
                 nc.vector.tensor_tensor(
-                    out=result[:, w, :],
+                    out=result[:, h, :],
                     in0=acc[:],
                     in1=offset[:].rearrange("p q n -> p (q n)"),
                     op=add,
@@ -190,14 +228,20 @@ def tile_edgemodel_pa_t_kernel(
             nc.scalar.activation(out=result[:], in_=result[:], func=relu)
             nc.sync.dma_start(
                 out=out_by_slot[:, r * ROUND_SLOTS : (r + 1) * ROUND_SLOTS, :],
-                in_=result[:].rearrange("p w (q n) -> p (w q) n", n=LATENT),
+                in_=result[:].rearrange("p h (q n) -> p (h q) n", n=LATENT),
             )
 
+        sort_round(0)
+        sort_round(1)
         transpose_round(0)
+        quantise_global()
+        sort_round(2)
         transpose_round(1)
         global_and_bias()
         multiply_round(0)
         for r in range(2, ROUNDS):
+            if r + 1 < ROUNDS:
+                sort_round(r + 1)
             transpose_round(r)
             multiply_round(r - 1)
             finish_round(r - 2)

@@ -63,7 +63,6 @@ def tile_edgemodel_pa_t_kernel(
         ctx.enter_context(tc.manual_schedule())
         const = ctx.enter_context(tc.tile_pool(name="const", bufs=1))
         x_pool = ctx.enter_context(tc.tile_pool(name="x", bufs=ROUNDS))
-        sorted_pool = ctx.enter_context(tc.tile_pool(name="sorted", bufs=4))
         grouped_pool = ctx.enter_context(tc.tile_pool(name="grouped", bufs=4))
         codes_pool = ctx.enter_context(tc.tile_pool(name="codes", bufs=9))
         result_pool = ctx.enter_context(tc.tile_pool(name="result", bufs=6))
@@ -81,11 +80,11 @@ def tile_edgemodel_pa_t_kernel(
         x_tiles = []
 
         def load_round(r):
-            x_tile = x_pool.tile([P, BIG, ROUND_SLOTS, FEATURES], BF16, name="x")
+            x_tile = x_pool.tile([P, ROUND_SLOTS, BIG, FEATURES], BF16, name="x", align_bytes=256)
             for s in range(BIG):
                 by_slot = inputs[s].rearrange("(p t) f -> p t f", t=SLOTS)
                 nc.sync.dma_start(
-                    out=x_tile[:, s, :, :],
+                    out=x_tile[:, :, s, :],
                     in_=by_slot[:, r * ROUND_SLOTS : (r + 1) * ROUND_SLOTS, :],
                 )
             x_tiles.append(x_tile)
@@ -148,30 +147,11 @@ def tile_edgemodel_pa_t_kernel(
                 op=add,
             )
 
-        sorted_tiles = []
-
-        def sort_round(r):
-            words = (
-                x_tiles[r][:]
-                .rearrange("p s t f -> p (s t f)")
-                .bitcast(F32)
-                .rearrange("p (s t i u) -> p u t s i", s=BIG, t=ROUND_SLOTS, u=2)
-            )
-            in_order = sorted_pool.tile([P, 2, ROUND_WORDS], F32)
-            for u in range(2):
-                nc.vector.tensor_copy(
-                    out=in_order[:, u, :].rearrange(
-                        "p (t s i) -> p t s i", t=ROUND_SLOTS, s=BIG
-                    ),
-                    in_=words[:, u],
-                )
-            sorted_tiles.append(in_order)
-
         quantised = []
 
         def transpose_round(r):
             operands = []
-            in_order = sorted_tiles[r]
+            words = x_tiles[r][:].rearrange("p t s f -> p (t s f)").bitcast(F32)
             for b in range(OPERANDS // 2):
                 flipped = flipped_psum.tile([P, 2, 2, P], F32)
                 for w in range(2):
@@ -179,7 +159,7 @@ def tile_edgemodel_pa_t_kernel(
                     for u in range(2):
                         nc.tensor.transpose(
                             flipped[:, w, u, :],
-                            in_order[:, u, j * P : (j + 1) * P],
+                            words[:, 2 * j * P + u : 2 * (j + 1) * P : 2],
                             identity[:],
                         )
                 grouped = grouped_pool.tile([P, 2 * P * PACK], BF16, align_bytes=64)
@@ -231,17 +211,12 @@ def tile_edgemodel_pa_t_kernel(
                 in_=result[:].rearrange("p h (q n) -> p (h q) n", n=LATENT),
             )
 
-        sort_round(0)
-        sort_round(1)
         transpose_round(0)
         quantise_global()
-        sort_round(2)
         transpose_round(1)
         global_and_bias()
         multiply_round(0)
         for r in range(2, ROUNDS):
-            if r + 1 < ROUNDS:
-                sort_round(r + 1)
             transpose_round(r)
             multiply_round(r - 1)
             finish_round(r - 2)

@@ -65,7 +65,7 @@ def tile_edgemodel_pa_t_kernel(
         x_pool = ctx.enter_context(tc.tile_pool(name="x", bufs=ROUNDS))
         grouped_pool = ctx.enter_context(tc.tile_pool(name="grouped", bufs=4))
         codes_pool = ctx.enter_context(tc.tile_pool(name="codes", bufs=9))
-        result_pool = ctx.enter_context(tc.tile_pool(name="result", bufs=6))
+        result_pool = ctx.enter_context(tc.tile_pool(name="result", bufs=ROUNDS))
         flipped_psum = ctx.enter_context(tc.psum_pool(name="flipped", bufs=4))
         acc_psum = ctx.enter_context(tc.psum_pool(name="acc", bufs=4))
 

@@ -205,7 +205,8 @@ def tile_edgemodel_pa_t_kernel(
 
         def finish_round(r):
             result = results[r]
-            nc.scalar.activation(out=result[:], in_=result[:], func=relu)
+            nc.vector.tensor_scalar_max(out=result[:, 0, :], in0=result[:, 0, :], scalar1=0.0)
+            nc.scalar.activation(out=result[:, 1, :], in_=result[:, 1, :], func=relu)
             nc.sync.dma_start(
                 out=out_by_slot[:, r * ROUND_SLOTS : (r + 1) * ROUND_SLOTS, :],
                 in_=result[:].rearrange("p h (q n) -> p (h q) n", n=LATENT),

@@ -90,6 +90,8 @@ def tile_edgemodel_pa_t_kernel(
             x_tiles.append(x_tile)
 
         load_round(0)
+        load_round(1)
+        load_round(2)
         words_by_piece = W1_words[0].bitcast(I32).rearrange("(s i) b -> i s b", s=PIECES)
         scales_by_piece = W1_scales[0].bitcast(I32).rearrange("(s r) b -> r s b", s=PIECES)
         for q, v0, vstep, s0, count in WEIGHT_LOADS:
@@ -102,7 +104,7 @@ def tile_edgemodel_pa_t_kernel(
                 out=w_scales[q * QUAD : q * QUAD + 4, variants, :].bitcast(I32),
                 in_=scales_by_piece[:, s0 : s0 + count, :],
             )
-        for r in range(1, ROUNDS):
+        for r in range(3, ROUNDS):
             load_round(r)
 
         g_rows = const.tile([P, PACK], BF16)
@@ -215,9 +217,12 @@ def tile_edgemodel_pa_t_kernel(
         transpose_round(0)
         quantise_global()
         transpose_round(1)
+        transpose_round(2)
         global_and_bias()
         multiply_round(0)
-        for r in range(2, ROUNDS):
+        multiply_round(1)
+        finish_round(0)
+        for r in range(3, ROUNDS):
             transpose_round(r)
             multiply_round(r - 1)
             finish_round(r - 2)

@@ -27,6 +27,7 @@ ROUND_SLOTS = 8
 ROUNDS = SLOTS // ROUND_SLOTS
 ROUND_WORDS = ROUND_SLOTS * BIG * HALF
 OPERANDS = ROUND_WORDS // P
+BANKS = OPERANDS // 2
 UNIT_SLOTS = 4
 UNITS = ROUND_SLOTS // UNIT_SLOTS
 VARIANTS = 7
@@ -63,7 +64,7 @@ def tile_edgemodel_pa_t_kernel(
         ctx.enter_context(tc.manual_schedule())
         const = ctx.enter_context(tc.tile_pool(name="const", bufs=1))
         x_pool = ctx.enter_context(tc.tile_pool(name="x", bufs=ROUNDS))
-        grouped_pool = ctx.enter_context(tc.tile_pool(name="grouped", bufs=4))
+        grouped_pool = ctx.enter_context(tc.tile_pool(name="grouped", bufs=6))
         codes_pool = ctx.enter_context(tc.tile_pool(name="codes", bufs=9))
         result_pool = ctx.enter_context(tc.tile_pool(name="result", bufs=ROUNDS))
         flipped_psum = ctx.enter_context(tc.psum_pool(name="flipped", bufs=4))
@@ -149,45 +150,46 @@ def tile_edgemodel_pa_t_kernel(
                 op=add,
             )
 
+        grouped_tiles = []
         quantised = []
 
-        def transpose_round(r):
-            operands = []
+        def flip_bank(r, b):
             words = x_tiles[r][:].rearrange("p t s f -> p (t s f)").bitcast(F32)
-            for b in range(OPERANDS // 2):
-                flipped = flipped_psum.tile([P, 2, 2, P], F32)
-                for w in range(2):
-                    j = 2 * b + w
-                    for u in range(2):
-                        nc.tensor.transpose(
-                            flipped[:, w, u, :],
-                            words[:, 2 * j * P + u : 2 * (j + 1) * P : 2],
-                            identity[:],
-                        )
-                grouped = grouped_pool.tile([P, 2 * P * PACK], BF16, align_bytes=64)
-                nc.scalar.copy(
-                    out=grouped[:].bitcast(F32).rearrange("k (w e u) -> k w e u", w=2, u=2),
-                    in_=flipped[:].rearrange("k w u e -> k w e u"),
-                )
-                codes = codes_pool.tile([P, 2 * P], U32, align_bytes=64)
-                plane = codes_pool.tile([P, 2 * P], U8, align_bytes=64)
-                nc.vector.quantize_mx(
-                    out=codes[:].bitcast(FP8X4), scales=plane[:], in_=grouped[:]
-                )
-                operands.append((codes, plane))
-            quantised.append(operands)
+            flipped = flipped_psum.tile([P, 2, 2, P], F32)
+            for w in range(2):
+                j = 2 * b + w
+                for u in range(2):
+                    nc.tensor.transpose(
+                        flipped[:, w, u, :],
+                        words[:, 2 * j * P + u : 2 * (j + 1) * P : 2],
+                        identity[:],
+                    )
+            grouped = grouped_pool.tile([P, 2 * P * PACK], BF16, align_bytes=64)
+            nc.scalar.copy(
+                out=grouped[:].bitcast(F32).rearrange("k (w e u) -> k w e u", w=2, u=2),
+                in_=flipped[:].rearrange("k w u e -> k w e u"),
+            )
+            grouped_tiles.append(grouped)
+
+        def quantise_bank(r, b):
+            codes = codes_pool.tile([P, 2 * P], U32, align_bytes=64)
+            plane = codes_pool.tile([P, 2 * P], U8, align_bytes=64)
+            nc.vector.quantize_mx(
+                out=codes[:].bitcast(FP8X4), scales=plane[:], in_=grouped_tiles[BANKS * r + b][:]
+            )
+            quantised.append((codes, plane))
 
         out_by_slot = out.rearrange("(p t) n -> p t n", t=SLOTS)
         results = []
+        sums = []
 
         def multiply_round(r):
-            result = result_pool.tile([P, UNITS, UNIT_SLOTS * LATENT], F32)
-            results.append(result)
             for h in range(UNITS):
                 acc = acc_psum.tile([P, UNIT_SLOTS * LATENT], F32)
+                sums.append(acc)
                 for operand, slot, variant, start, stop in PASSES:
                     j = 3 * h + operand
-                    codes, plane = quantised[r][j // 2]
+                    codes, plane = quantised[BANKS * r + j // 2]
                     edges = slice((j % 2) * P, (j % 2 + 1) * P)
                     nc.tensor.matmul_mx(
                         out=acc[:, slot * LATENT : (slot + 1) * LATENT],
@@ -198,34 +200,47 @@ def tile_edgemodel_pa_t_kernel(
                         start=start,
                         stop=stop,
                     )
+
+        def add_round(r):
+            result = result_pool.tile([P, UNITS, UNIT_SLOTS * LATENT], F32)
+            results.append(result)
+            for h in range(UNITS):
                 nc.vector.tensor_tensor(
                     out=result[:, h, :],
-                    in0=acc[:],
+                    in0=sums[UNITS * r + h][:],
                     in1=offset[:].rearrange("p q n -> p (q n)"),
                     op=add,
                 )
+            nc.vector.tensor_scalar_max(out=result[:, 0, :], in0=result[:, 0, :], scalar1=0.0)
 
         def finish_round(r):
             result = results[r]
-            nc.vector.tensor_scalar_max(out=result[:, 0, :], in0=result[:, 0, :], scalar1=0.0)
             nc.scalar.activation(out=result[:, 1, :], in_=result[:, 1, :], func=relu)
             nc.sync.dma_start(
                 out=out_by_slot[:, r * ROUND_SLOTS : (r + 1) * ROUND_SLOTS, :],
                 in_=result[:].rearrange("p h (q n) -> p (h q) n", n=LATENT),
             )
 
-        transpose_round(0)
-        quantise_global()
-        transpose_round(1)
-        transpose_round(2)
-        global_and_bias()
-        multiply_round(0)
-        multiply_round(1)
-        finish_round(0)
-        for r in range(3, ROUNDS):
-            transpose_round(r)
-            multiply_round(r - 1)
-            finish_round(r - 2)
-        multiply_round(ROUNDS - 1)
-        finish_round(ROUNDS - 2)
-        finish_round(ROUNDS - 1)
+        for i in range(ROUNDS + 2):
+            if 1 <= i <= ROUNDS:
+                quantise_bank(i - 1, BANKS - 1)
+            if i == 3:
+                add_round(0)
+            if i >= 3:
+                add_round(i - 2)
+            if i < ROUNDS:
+                for b in range(BANKS):
+                    flip_bank(i, b)
+                    if b < BANKS - 1:
+                        quantise_bank(i, b)
+            if i == 0:
+                quantise_global()
+            if i == 2:
+                global_and_bias()
+                multiply_round(0)
+            if 2 <= i <= ROUNDS:
+                multiply_round(i - 1)
+            if i == 3:
+                finish_round(0)
+            if i >= 3:
+                finish_round(i - 2)

@@ -109,13 +109,21 @@ def tile_edgemodel_pa_t_kernel(
             load_round(r)
 
         g_rows = const.tile([P, PACK], BF16)
-        for q in range(QUADS):
-            nc.scalar.dma_start(
-                out=g_rows[q * QUAD : (q + 1) * QUAD, :],
-                in_=global_attr.rearrange("o (i t) -> (o i) t", t=PACK),
-            )
-        bias_rows = const.tile([P, LATENT], BF16)
-        nc.scalar.dma_start(out=bias_rows[:], in_=b1.partition_broadcast(P))
+        nc.vector.memset(g_rows[:], 0.0)
+        nc.scalar.dma_start(
+            out=g_rows[0:QUAD, :], in_=global_attr.rearrange("o (i t) -> (o i) t", t=PACK)
+        )
+        bias_top = const.tile([P, LATENT], BF16)
+        nc.vector.memset(bias_top[:], 0.0)
+        nc.scalar.dma_start(out=bias_top[0:1, :], in_=b1.rearrange("(o n) -> o n", o=1))
+        ones = const.tile([P, P], BF16)
+        nc.vector.memset(ones[:], 1.0)
+        g_acc = acc_psum.tile([P, UNIT_SLOTS * LATENT], F32, tag="acc")
+        nc.tensor.matmul(
+            out=g_acc[:, LATENT : 2 * LATENT], lhsT=ones[:], rhs=bias_top[:], start=True, stop=True
+        )
+        bias_rows = const.tile([P, LATENT], F32)
+        nc.vector.tensor_copy(out=bias_rows[:], in_=g_acc[:, LATENT : 2 * LATENT])
 
         g_grouped = const.tile([P, P, PACK], BF16, align_bytes=64)
         g_codes = const.tile([P, P], U32, align_bytes=64)
@@ -133,7 +141,6 @@ def tile_edgemodel_pa_t_kernel(
             )
 
         def global_and_bias():
-            g_acc = acc_psum.tile([P, UNIT_SLOTS * LATENT], F32, tag="acc")
             nc.tensor.matmul_mx(
                 out=g_acc[:, 0:LATENT],
                 lhsT=g_codes[:].bitcast(FP8X4),

@@ -35,20 +35,12 @@ VARIANTS = 7
 FLOPS = 2 * EDGES * PIECES * FEATURES * LATENT
 
 PASSES = (
-    (0, 0, 0, True, True),
-    (0, 1, 1, True, False),
-    (1, 1, 2, False, True),
-    (1, 2, 3, True, False),
-    (2, 2, 4, False, True),
-    (2, 3, 5, True, True),
-)
-WEIGHT_LOADS = (
-    (0, 0, 2, 0, 4),
-    (3, 1, 2, 0, 3),
-    (1, 0, 2, 1, 2),
-    (1, 5, 1, 0, 1),
-    (2, 3, 2, 0, 2),
-    (2, 0, 1, 2, 1),
+    (0, 0, True, True),
+    (0, 1, True, False),
+    (1, 1, False, True),
+    (1, 2, True, False),
+    (2, 2, False, True),
+    (2, 3, True, True),
 )
 
 
@@ -80,33 +72,41 @@ def tile_edgemodel_pa_t_kernel(
 
         x_tiles = []
 
-        def load_round(r):
-            x_tile = x_pool.tile([P, ROUND_SLOTS, BIG, FEATURES], BF16, name="x", align_bytes=256)
-            for s in range(BIG):
-                by_slot = inputs[s].rearrange("(p t) f -> p t f", t=SLOTS)
-                nc.sync.dma_start(
-                    out=x_tile[:, :, s, :],
-                    in_=by_slot[:, r * ROUND_SLOTS : (r + 1) * ROUND_SLOTS, :],
+        def load_input(r, s):
+            if s == 0:
+                x_tile = x_pool.tile(
+                    [P, ROUND_SLOTS, BIG, FEATURES], BF16, name="x", align_bytes=256
                 )
-            x_tiles.append(x_tile)
+                x_tiles.append(x_tile)
+            by_slot = inputs[s].rearrange("(p t) f -> p t f", t=SLOTS)
+            nc.sync.dma_start(
+                out=x_tiles[r][:, :, s, :],
+                in_=by_slot[:, r * ROUND_SLOTS : (r + 1) * ROUND_SLOTS, :],
+            )
 
-        load_round(0)
-        load_round(1)
-        load_round(2)
         words_by_piece = W1_words[0].bitcast(I32).rearrange("(s i) b -> i s b", s=PIECES)
         scales_by_piece = W1_scales[0].bitcast(I32).rearrange("(s r) b -> r s b", s=PIECES)
-        for q, v0, vstep, s0, count in WEIGHT_LOADS:
-            variants = slice(v0, v0 + vstep * (count - 1) + 1, vstep)
-            nc.sync.dma_start(
-                out=w_words[q * QUAD : (q + 1) * QUAD, variants, :].bitcast(I32),
-                in_=words_by_piece[:, s0 : s0 + count, :],
-            )
-            nc.sync.dma_start(
-                out=w_scales[q * QUAD : q * QUAD + 4, variants, :].bitcast(I32),
-                in_=scales_by_piece[:, s0 : s0 + count, :],
-            )
-        for r in range(3, ROUNDS):
-            load_round(r)
+
+        def load_weights(q, scales):
+            count = PIECES if q == 0 else BIG
+            variants = slice(3 - q, 3 - q + count)
+            if scales:
+                nc.sync.dma_start(
+                    out=w_scales[q * QUAD : q * QUAD + 4, variants, :].bitcast(I32),
+                    in_=scales_by_piece[:, 0:count, :],
+                )
+            else:
+                nc.sync.dma_start(
+                    out=w_words[q * QUAD : (q + 1) * QUAD, variants, :].bitcast(I32),
+                    in_=words_by_piece[:, 0:count, :],
+                )
+
+        for r in range(ROUNDS):
+            for s in range(BIG):
+                k = BIG * (r - 1) + s
+                if 0 <= k < 2 * QUADS:
+                    load_weights(k // 2, k % 2 == 1)
+                load_input(r, s)
 
         g_rows = const.tile([P, PACK], BF16)
         nc.vector.memset(g_rows[:], 0.0)
@@ -118,12 +118,7 @@ def tile_edgemodel_pa_t_kernel(
         nc.scalar.dma_start(out=bias_top[0:1, :], in_=b1.rearrange("(o n) -> o n", o=1))
         ones = const.tile([P, P], BF16)
         nc.vector.memset(ones[:], 1.0)
-        g_acc = acc_psum.tile([P, UNIT_SLOTS * LATENT], F32, tag="acc")
-        nc.tensor.matmul(
-            out=g_acc[:, LATENT : 2 * LATENT], lhsT=ones[:], rhs=bias_top[:], start=True, stop=True
-        )
         bias_rows = const.tile([P, LATENT], F32)
-        nc.vector.tensor_copy(out=bias_rows[:], in_=g_acc[:, LATENT : 2 * LATENT])
 
         g_grouped = const.tile([P, P, PACK], BF16, align_bytes=64)
         g_codes = const.tile([P, P], U32, align_bytes=64)
@@ -141,6 +136,12 @@ def tile_edgemodel_pa_t_kernel(
             )
 
         def global_and_bias():
+            b_acc = acc_psum.tile([P, UNIT_SLOTS * LATENT], F32, tag="acc")
+            nc.tensor.matmul(
+                out=b_acc[:, 0:LATENT], lhsT=ones[:], rhs=bias_top[:], start=True, stop=True
+            )
+            nc.vector.tensor_copy(out=bias_rows[:], in_=b_acc[:, 0:LATENT])
+            g_acc = acc_psum.tile([P, UNIT_SLOTS * LATENT], F32, tag="acc")
             nc.tensor.matmul_mx(
                 out=g_acc[:, 0:LATENT],
                 lhsT=g_codes[:].bitcast(FP8X4),
@@ -194,7 +195,8 @@ def tile_edgemodel_pa_t_kernel(
             for h in range(UNITS):
                 acc = acc_psum.tile([P, UNIT_SLOTS * LATENT], F32)
                 sums.append(acc)
-                for operand, slot, variant, start, stop in PASSES:
+                for operand, slot, start, stop in PASSES:
+                    variant = 3 - 3 * slot + 4 * operand
                     j = 3 * h + operand
                     codes, plane = quantised[BANKS * r + j // 2]
                     edges = slice((j % 2) * P, (j % 2 + 1) * P)

@@ -72,16 +72,11 @@ def tile_edgemodel_pa_t_kernel(
 
         x_tiles = []
 
-        def load_input(r, s):
-            if s == 0:
-                x_tile = x_pool.tile(
-                    [P, ROUND_SLOTS, BIG, FEATURES], BF16, name="x", align_bytes=256
-                )
-                x_tiles.append(x_tile)
+        def load_input(r, s, first, count):
             by_slot = inputs[s].rearrange("(p t) f -> p t f", t=SLOTS)
             nc.sync.dma_start(
-                out=x_tiles[r][:, :, s, :],
-                in_=by_slot[:, r * ROUND_SLOTS : (r + 1) * ROUND_SLOTS, :],
+                out=x_tiles[r][:, first : first + count, s, :],
+                in_=by_slot[:, r * ROUND_SLOTS + first : r * ROUND_SLOTS + first + count, :],
             )
 
         words_by_piece = W1_words[0].bitcast(I32).rearrange("(s i) b -> i s b", s=PIECES)
@@ -102,11 +97,18 @@ def tile_edgemodel_pa_t_kernel(
                 )
 
         for r in range(ROUNDS):
-            for s in range(BIG):
-                k = BIG * (r - 1) + s
-                if 0 <= k < 2 * QUADS:
-                    load_weights(k // 2, k % 2 == 1)
-                load_input(r, s)
+            x_tile = x_pool.tile([P, ROUND_SLOTS, BIG, FEATURES], BF16, name="x", align_bytes=256)
+            x_tiles.append(x_tile)
+            if r == 0:
+                for h in range(UNITS):
+                    for s in range(BIG):
+                        load_input(r, s, h * UNIT_SLOTS, UNIT_SLOTS)
+            else:
+                for s in range(BIG):
+                    k = BIG * (r - 1) + s
+                    if k < 2 * QUADS:
+                        load_weights(k // 2, k % 2 == 1)
+                    load_input(r, s, 0, ROUND_SLOTS)
 
         g_rows = const.tile([P, PACK], BF16)
         nc.vector.memset(g_rows[:], 0.0)
@@ -210,46 +212,69 @@ def tile_edgemodel_pa_t_kernel(
                         stop=stop,
                     )
 
-        def add_round(r):
-            result = result_pool.tile([P, UNITS, UNIT_SLOTS * LATENT], F32)
-            results.append(result)
-            for h in range(UNITS):
-                nc.vector.tensor_tensor(
-                    out=result[:, h, :],
-                    in0=sums[UNITS * r + h][:],
-                    in1=offset[:].rearrange("p q n -> p (q n)"),
-                    op=add,
-                )
-            nc.vector.tensor_scalar_max(out=result[:, 0, :], in0=result[:, 0, :], scalar1=0.0)
-
-        def finish_round(r):
-            result = results[r]
-            nc.scalar.activation(out=result[:, 1, :], in_=result[:, 1, :], func=relu)
-            nc.sync.dma_start(
-                out=out_by_slot[:, r * ROUND_SLOTS : (r + 1) * ROUND_SLOTS, :],
-                in_=result[:].rearrange("p h (q n) -> p (h q) n", n=LATENT),
+        def add_bank(r, h):
+            if h == 0:
+                result = result_pool.tile([P, UNITS, UNIT_SLOTS * LATENT], F32)
+                results.append(result)
+            nc.vector.tensor_tensor(
+                out=results[r][:, h, :],
+                in0=sums[UNITS * r + h][:],
+                in1=offset[:].rearrange("p q n -> p (q n)"),
+                op=add,
             )
 
-        for i in range(ROUNDS + 2):
-            if 1 <= i <= ROUNDS:
+        def add_round(r):
+            for h in range(UNITS):
+                add_bank(r, h)
+            nc.vector.tensor_scalar_max(
+                out=results[r][:, 0, :], in0=results[r][:, 0, :], scalar1=0.0
+            )
+
+        def scalar_relu(r, h):
+            nc.scalar.activation(out=results[r][:, h, :], in_=results[r][:, h, :], func=relu)
+
+        def store(r, h, count):
+            first = r * ROUND_SLOTS + h * UNIT_SLOTS
+            nc.sync.dma_start(
+                out=out_by_slot[:, first : first + count * UNIT_SLOTS, :],
+                in_=results[r][:, h : h + count, :].rearrange("p h (q n) -> p (h q) n", n=LATENT),
+            )
+
+        def finish_round(r):
+            scalar_relu(r, 1)
+            store(r, 0, UNITS)
+
+        for i in range(ROUNDS):
+            if i >= 1:
                 quantise_bank(i - 1, BANKS - 1)
             if i == 3:
                 add_round(0)
             if i >= 3:
                 add_round(i - 2)
-            if i < ROUNDS:
-                for b in range(BANKS):
-                    flip_bank(i, b)
-                    if b < BANKS - 1:
-                        quantise_bank(i, b)
+            for b in range(BANKS):
+                flip_bank(i, b)
+                if b < BANKS - 1:
+                    quantise_bank(i, b)
             if i == 0:
                 quantise_global()
             if i == 2:
                 global_and_bias()
                 multiply_round(0)
-            if 2 <= i <= ROUNDS:
+            if i >= 2:
                 multiply_round(i - 1)
             if i == 3:
                 finish_round(0)
             if i >= 3:
                 finish_round(i - 2)
+
+        add_bank(ROUNDS - 2, 0)
+        quantise_bank(ROUNDS - 1, BANKS - 1)
+        multiply_round(ROUNDS - 1)
+        scalar_relu(ROUNDS - 2, 0)
+        add_bank(ROUNDS - 2, 1)
+        scalar_relu(ROUNDS - 2, 1)
+        store(ROUNDS - 2, 0, UNITS)
+        for h in range(UNITS):
+            add_bank(ROUNDS - 1, h)
+            scalar_relu(ROUNDS - 1, h)
+            store(ROUNDS - 1, h, 1)

@@ -30,18 +30,20 @@ OPERANDS = ROUND_WORDS // P
 BANKS = OPERANDS // 2
 UNIT_SLOTS = 4
 UNITS = ROUND_SLOTS // UNIT_SLOTS
-VARIANTS = 7
+VARIANTS = 10
 
 FLOPS = 2 * EDGES * PIECES * FEATURES * LATENT
 
 PASSES = (
-    (0, 0, True, True),
-    (0, 1, True, False),
-    (1, 1, False, True),
-    (1, 2, True, False),
-    (2, 2, False, True),
-    (2, 3, True, True),
+    (0, 0, 3, True, True),
+    (0, 1, 7, True, False),
+    (1, 1, 8, False, True),
+    (1, 2, 1, True, False),
+    (2, 2, 5, False, True),
+    (2, 3, 9, True, True),
 )
+GLOBAL_VARIANT = 6
+COMPOSED = ((7, 3, 2), (8, 0, 1), (8, 1, 0), (9, 1, 2), (9, 2, 1), (9, 3, 0))
 
 
 def tile_edgemodel_pa_t_kernel(
@@ -55,7 +57,7 @@ def tile_edgemodel_pa_t_kernel(
     with ExitStack() as ctx:
         ctx.enter_context(tc.manual_schedule())
         const = ctx.enter_context(tc.tile_pool(name="const", bufs=1))
-        x_pool = ctx.enter_context(tc.tile_pool(name="x", bufs=ROUNDS))
+        x_pool = ctx.enter_context(tc.tile_pool(name="x", bufs=1))
         grouped_pool = ctx.enter_context(tc.tile_pool(name="grouped", bufs=6))
         codes_pool = ctx.enter_context(tc.tile_pool(name="codes", bufs=9))
         result_pool = ctx.enter_context(tc.tile_pool(name="result", bufs=ROUNDS))
@@ -70,13 +72,41 @@ def tile_edgemodel_pa_t_kernel(
         identity = const.tile([P, P], F32)
         make_identity(nc, identity[:])
 
-        x_tiles = []
+        x_all = x_pool.tile([P, SLOTS * BIG * FEATURES], BF16, name="x", align_bytes=256)
+        two_slots = 2 * BIG * FEATURES
+        x_by_slot = x_all[:].rearrange("p (t c) -> p t c", c=BIG * FEATURES)
+        x_by_two = x_all[:].rearrange("p (m c) -> p m c", c=two_slots)
+        x_shifted = x_all[
+            :, two_slots - FEATURES : two_slots - FEATURES + (SLOTS // 2 - 1) * two_slots
+        ].rearrange("p (m c) -> p m c", c=two_slots)
+        in_by_slot = [a.rearrange("(p t) f -> p t f", t=SLOTS) for a in inputs]
 
-        def load_input(r, s, first, count):
-            by_slot = inputs[s].rearrange("(p t) f -> p t f", t=SLOTS)
+        def load_one(s, t, chunk):
             nc.sync.dma_start(
-                out=x_tiles[r][:, first : first + count, s, :],
-                in_=by_slot[:, r * ROUND_SLOTS + first : r * ROUND_SLOTS + first + count, :],
+                out=x_all[:, chunk * FEATURES : (chunk + 1) * FEATURES], in_=in_by_slot[s][:, t, :]
+            )
+
+        def load_input(s, first, count):
+            if s == 1:
+                nc.sync.dma_start(
+                    out=x_by_slot[:, first : first + count, FEATURES : 2 * FEATURES],
+                    in_=in_by_slot[s][:, first : first + count, :],
+                )
+                return
+            m = first // 2
+            if s == 2:
+                pairs = count // 2
+                line = x_by_two[:, m : m + pairs, 2 * FEATURES : 4 * FEATURES]
+                start = first
+            else:
+                pairs = min(count // 2, SLOTS // 2 - 1 - m)
+                line = x_shifted[:, m : m + pairs, 0 : 2 * FEATURES]
+                start = first + 1
+            nc.sync.dma_start(
+                out=line,
+                in_=in_by_slot[s][:, start : start + 2 * pairs, :].rearrange(
+                    "p (m two) f -> p m (two f)", two=2
+                ),
             )
 
         words_by_piece = W1_words[0].bitcast(I32).rearrange("(s i) b -> i s b", s=PIECES)
@@ -96,19 +126,27 @@ def tile_edgemodel_pa_t_kernel(
                     in_=words_by_piece[:, 0:count, :],
                 )
 
-        for r in range(ROUNDS):
-            x_tile = x_pool.tile([P, ROUND_SLOTS, BIG, FEATURES], BF16, name="x", align_bytes=256)
-            x_tiles.append(x_tile)
-            if r == 0:
-                for h in range(UNITS):
-                    for s in range(BIG):
-                        load_input(r, s, h * UNIT_SLOTS, UNIT_SLOTS)
-            else:
-                for s in range(BIG):
-                    k = BIG * (r - 1) + s
-                    if k < 2 * QUADS:
-                        load_weights(k // 2, k % 2 == 1)
-                    load_input(r, s, 0, ROUND_SLOTS)
+        load_one(0, 0, 0)
+        for h in range(UNITS):
+            for s in range(BIG):
+                load_input(s, h * UNIT_SLOTS, UNIT_SLOTS)
+        for r in range(1, ROUNDS):
+            for s in range(BIG):
+                k = BIG * (r - 1) + s
+                if k < 2 * QUADS:
+                    load_weights(k // 2, k % 2 == 1)
+                load_input(s, r * ROUND_SLOTS, ROUND_SLOTS)
+                if s == 0 and r == ROUNDS - 1:
+                    load_one(0, SLOTS - 1, SLOTS * BIG - 1)
+
+        def compose_variants():
+            for variant, q, s in COMPOSED:
+                rows = slice(q * QUAD, (q + 1) * QUAD)
+                for plane in (w_words, w_scales):
+                    nc.vector.tensor_copy(
+                        out=plane[rows, variant, :].bitcast(I32),
+                        in_=plane[rows, 3 - q + s, :].bitcast(I32),
+                    )
 
         g_rows = const.tile([P, PACK], BF16)
         nc.vector.memset(g_rows[:], 0.0)
@@ -148,8 +186,8 @@ def tile_edgemodel_pa_t_kernel(
                 out=g_acc[:, 0:LATENT],
                 lhsT=g_codes[:].bitcast(FP8X4),
                 lhsT_scale=g_plane[:],
-                rhs=w_words[:, VARIANTS - 1, :].bitcast(FP4X4),
-                rhs_scale=w_scales[:, VARIANTS - 1, :],
+                rhs=w_words[:, GLOBAL_VARIANT, :].bitcast(FP4X4),
+                rhs_scale=w_scales[:, GLOBAL_VARIANT, :],
                 start=True,
                 stop=True,
             )
@@ -164,10 +202,10 @@ def tile_edgemodel_pa_t_kernel(
         quantised = []
 
         def flip_bank(r, b):
-            words = x_tiles[r][:].rearrange("p t s f -> p (t s f)").bitcast(F32)
+            words = x_all[:].bitcast(F32)
             flipped = flipped_psum.tile([P, 2, 2, P], F32)
             for w in range(2):
-                j = 2 * b + w
+                j = OPERANDS * r + 2 * b + w
                 for u in range(2):
                     nc.tensor.transpose(
                         flipped[:, w, u, :],
@@ -197,8 +235,7 @@ def tile_edgemodel_pa_t_kernel(
             for h in range(UNITS):
                 acc = acc_psum.tile([P, UNIT_SLOTS * LATENT], F32)
                 sums.append(acc)
-                for operand, slot, start, stop in PASSES:
-                    variant = 3 - 3 * slot + 4 * operand
+                for operand, slot, variant, start, stop in PASSES:
                     j = 3 * h + operand
                     codes, plane = quantised[BANKS * r + j // 2]
                     edges = slice((j % 2) * P, (j % 2 + 1) * P)
@@ -258,6 +295,7 @@ def tile_edgemodel_pa_t_kernel(
             if i == 0:
                 quantise_global()
             if i == 2:
+                compose_variants()
                 global_and_bias()
                 multiply_round(0)
             if i >= 2:

from contextlib import ExitStack

import concourse.mybir as mybir
from concourse.masks import make_identity

BF16 = mybir.dt.bfloat16
F32 = mybir.dt.float32
I32 = mybir.dt.int32
U32 = mybir.dt.uint32
U8 = mybir.dt.uint8
FP8X4 = mybir.dt.float8_e4m3fn_x4
FP4X4 = mybir.dt.float4_e2m1fn_x4

P = 128
EDGES = 16384
FEATURES = 128
LATENT = 128
PIECES = 4
BIG = 3
PACK = 4
QUADS = 4
QUAD = P // QUADS
SLOTS = EDGES // P
WORDS = FEATURES // 2
HALF = WORDS // 2
ROUND_SLOTS = 8
ROUNDS = SLOTS // ROUND_SLOTS
ROUND_WORDS = ROUND_SLOTS * BIG * HALF
OPERANDS = ROUND_WORDS // P
BANKS = OPERANDS // 2
UNIT_SLOTS = 4
UNITS = ROUND_SLOTS // UNIT_SLOTS
VARIANTS = 10

FLOPS = 2 * EDGES * PIECES * FEATURES * LATENT

PASSES = (
    (0, 0, 3, True, True),
    (0, 1, 7, True, False),
    (1, 1, 8, False, True),
    (1, 2, 1, True, False),
    (2, 2, 5, False, True),
    (2, 3, 9, True, True),
)
GLOBAL_VARIANT = 6
COMPOSED = ((7, 3, 2), (8, 0, 1), (8, 1, 0), (9, 1, 2), (9, 2, 1), (9, 3, 0))


def tile_edgemodel_pa_t_kernel(
    tc, receiver, sender, edge_attr, global_attr, W1_words, W1_scales, b1, out
):
    nc = tc.nc
    inputs = (receiver, sender, edge_attr)
    add = mybir.AluOpType.add
    relu = mybir.ActivationFunctionType.Relu

    with ExitStack() as ctx:
        ctx.enter_context(tc.manual_schedule())
        const = ctx.enter_context(tc.tile_pool(name="const", bufs=1))
        x_pool = ctx.enter_context(tc.tile_pool(name="x", bufs=1))
        grouped_pool = ctx.enter_context(tc.tile_pool(name="grouped", bufs=6))
        codes_pool = ctx.enter_context(tc.tile_pool(name="codes", bufs=9))
        result_pool = ctx.enter_context(tc.tile_pool(name="result", bufs=ROUNDS))
        flipped_psum = ctx.enter_context(tc.psum_pool(name="flipped", bufs=4))
        acc_psum = ctx.enter_context(tc.psum_pool(name="acc", bufs=4))

        w_words = const.tile([P, VARIANTS, 2 * LATENT], U8, align_bytes=64)
        w_scales = const.tile([P, VARIANTS, LATENT], U8, align_bytes=64)
        nc.vector.memset(w_words[:].rearrange("p s b -> p (s b)").bitcast(I32), 0)
        nc.vector.memset(w_scales[:].rearrange("p s b -> p (s b)").bitcast(I32), 0)

        identity = const.tile([P, P], F32)
        make_identity(nc, identity[:])

        x_all = x_pool.tile([P, SLOTS * BIG * FEATURES], BF16, name="x", align_bytes=256)
        two_slots = 2 * BIG * FEATURES
        x_by_slot = x_all[:].rearrange("p (t c) -> p t c", c=BIG * FEATURES)
        x_by_two = x_all[:].rearrange("p (m c) -> p m c", c=two_slots)
        x_shifted = x_all[
            :, two_slots - FEATURES : two_slots - FEATURES + (SLOTS // 2 - 1) * two_slots
        ].rearrange("p (m c) -> p m c", c=two_slots)
        in_by_slot = [a.rearrange("(p t) f -> p t f", t=SLOTS) for a in inputs]

        def load_one(s, t, chunk):
            nc.sync.dma_start(
                out=x_all[:, chunk * FEATURES : (chunk + 1) * FEATURES], in_=in_by_slot[s][:, t, :]
            )

        def load_input(s, first, count):
            if s == 1:
                nc.sync.dma_start(
                    out=x_by_slot[:, first : first + count, FEATURES : 2 * FEATURES],
                    in_=in_by_slot[s][:, first : first + count, :],
                )
                return
            m = first // 2
            if s == 2:
                pairs = count // 2
                line = x_by_two[:, m : m + pairs, 2 * FEATURES : 4 * FEATURES]
                start = first
            else:
                pairs = min(count // 2, SLOTS // 2 - 1 - m)
                line = x_shifted[:, m : m + pairs, 0 : 2 * FEATURES]
                start = first + 1
            nc.sync.dma_start(
                out=line,
                in_=in_by_slot[s][:, start : start + 2 * pairs, :].rearrange(
                    "p (m two) f -> p m (two f)", two=2
                ),
            )

        words_by_piece = W1_words[0].bitcast(I32).rearrange("(s i) b -> i s b", s=PIECES)
        scales_by_piece = W1_scales[0].bitcast(I32).rearrange("(s r) b -> r s b", s=PIECES)

        def load_weights(q, scales):
            count = PIECES if q == 0 else BIG
            variants = slice(3 - q, 3 - q + count)
            if scales:
                nc.sync.dma_start(
                    out=w_scales[q * QUAD : q * QUAD + 4, variants, :].bitcast(I32),
                    in_=scales_by_piece[:, 0:count, :],
                )
            else:
                nc.sync.dma_start(
                    out=w_words[q * QUAD : (q + 1) * QUAD, variants, :].bitcast(I32),
                    in_=words_by_piece[:, 0:count, :],
                )

        load_one(0, 0, 0)
        for h in range(UNITS):
            for s in range(BIG):
                load_input(s, h * UNIT_SLOTS, UNIT_SLOTS)
        for r in range(1, ROUNDS):
            for s in range(BIG):
                k = BIG * (r - 1) + s
                if k < 2 * QUADS:
                    load_weights(k // 2, k % 2 == 1)
                load_input(s, r * ROUND_SLOTS, ROUND_SLOTS)
                if s == 0 and r == ROUNDS - 1:
                    load_one(0, SLOTS - 1, SLOTS * BIG - 1)

        def compose_variants():
            for variant, q, s in COMPOSED:
                rows = slice(q * QUAD, (q + 1) * QUAD)
                for plane in (w_words, w_scales):
                    nc.vector.tensor_copy(
                        out=plane[rows, variant, :].bitcast(I32),
                        in_=plane[rows, 3 - q + s, :].bitcast(I32),
                    )

        g_rows = const.tile([P, PACK], BF16)
        nc.vector.memset(g_rows[:], 0.0)
        nc.scalar.dma_start(
            out=g_rows[0:QUAD, :], in_=global_attr.rearrange("o (i t) -> (o i) t", t=PACK)
        )
        bias_top = const.tile([P, LATENT], BF16)
        nc.vector.memset(bias_top[:], 0.0)
        nc.scalar.dma_start(out=bias_top[0:1, :], in_=b1.rearrange("(o n) -> o n", o=1))
        ones = const.tile([P, P], BF16)
        nc.vector.memset(ones[:], 1.0)
        bias_rows = const.tile([P, LATENT], F32)

        g_grouped = const.tile([P, P, PACK], BF16, align_bytes=64)
        g_codes = const.tile([P, P], U32, align_bytes=64)
        g_plane = const.tile([P, P], U8, align_bytes=64)
        offset = const.tile([P, UNIT_SLOTS, LATENT], F32)

        def quantise_global():
            nc.vector.tensor_copy(
                out=g_grouped[:], in_=g_rows[:].unsqueeze(1).to_broadcast([P, P, PACK])
            )
            nc.vector.quantize_mx(
                out=g_codes[:].bitcast(FP8X4),
                scales=g_plane[:],
                in_=g_grouped[:].rearrange("p c t -> p (c t)"),
            )

        def global_and_bias():
            b_acc = acc_psum.tile([P, UNIT_SLOTS * LATENT], F32, tag="acc")
            nc.tensor.matmul(
                out=b_acc[:, 0:LATENT], lhsT=ones[:], rhs=bias_top[:], start=True, stop=True
            )
            nc.vector.tensor_copy(out=bias_rows[:], in_=b_acc[:, 0:LATENT])
            g_acc = acc_psum.tile([P, UNIT_SLOTS * LATENT], F32, tag="acc")
            nc.tensor.matmul_mx(
                out=g_acc[:, 0:LATENT],
                lhsT=g_codes[:].bitcast(FP8X4),
                lhsT_scale=g_plane[:],
                rhs=w_words[:, GLOBAL_VARIANT, :].bitcast(FP4X4),
                rhs_scale=w_scales[:, GLOBAL_VARIANT, :],
                start=True,
                stop=True,
            )
            nc.vector.tensor_tensor(
                out=offset[:],
                in0=g_acc[:, 0:LATENT].unsqueeze(1).to_broadcast([P, UNIT_SLOTS, LATENT]),
                in1=bias_rows[:].unsqueeze(1).to_broadcast([P, UNIT_SLOTS, LATENT]),
                op=add,
            )

        grouped_tiles = []
        quantised = []

        def flip_bank(r, b):
            words = x_all[:].bitcast(F32)
            flipped = flipped_psum.tile([P, 2, 2, P], F32)
            for w in range(2):
                j = OPERANDS * r + 2 * b + w
                for u in range(2):
                    nc.tensor.transpose(
                        flipped[:, w, u, :],
                        words[:, 2 * j * P + u : 2 * (j + 1) * P : 2],
                        identity[:],
                    )
            grouped = grouped_pool.tile([P, 2 * P * PACK], BF16, align_bytes=64)
            nc.scalar.copy(
                out=grouped[:].bitcast(F32).rearrange("k (w e u) -> k w e u", w=2, u=2),
                in_=flipped[:].rearrange("k w u e -> k w e u"),
            )
            grouped_tiles.append(grouped)

        def quantise_bank(r, b):
            codes = codes_pool.tile([P, 2 * P], U32, align_bytes=64)
            plane = codes_pool.tile([P, 2 * P], U8, align_bytes=64)
            nc.vector.quantize_mx(
                out=codes[:].bitcast(FP8X4), scales=plane[:], in_=grouped_tiles[BANKS * r + b][:]
            )
            quantised.append((codes, plane))

        out_by_slot = out.rearrange("(p t) n -> p t n", t=SLOTS)
        results = []
        sums = []

        def multiply_round(r):
            for h in range(UNITS):
                acc = acc_psum.tile([P, UNIT_SLOTS * LATENT], F32)
                sums.append(acc)
                for operand, slot, variant, start, stop in PASSES:
                    j = 3 * h + operand
                    codes, plane = quantised[BANKS * r + j // 2]
                    edges = slice((j % 2) * P, (j % 2 + 1) * P)
                    nc.tensor.matmul_mx(
                        out=acc[:, slot * LATENT : (slot + 1) * LATENT],
                        lhsT=codes[:, edges].bitcast(FP8X4),
                        lhsT_scale=plane[:, edges],
                        rhs=w_words[:, variant, :].bitcast(FP4X4),
                        rhs_scale=w_scales[:, variant, :],
                        start=start,
                        stop=stop,
                    )

        def add_bank(r, h):
            if h == 0:
                result = result_pool.tile([P, UNITS, UNIT_SLOTS * LATENT], F32)
                results.append(result)
            nc.vector.tensor_tensor(
                out=results[r][:, h, :],
                in0=sums[UNITS * r + h][:],
                in1=offset[:].rearrange("p q n -> p (q n)"),
                op=add,
            )

        def add_round(r):
            for h in range(UNITS):
                add_bank(r, h)
            nc.vector.tensor_scalar_max(
                out=results[r][:, 0, :], in0=results[r][:, 0, :], scalar1=0.0
            )

        def scalar_relu(r, h):
            nc.scalar.activation(out=results[r][:, h, :], in_=results[r][:, h, :], func=relu)

        def store(r, h, count):
            first = r * ROUND_SLOTS + h * UNIT_SLOTS
            nc.sync.dma_start(
                out=out_by_slot[:, first : first + count * UNIT_SLOTS, :],
                in_=results[r][:, h : h + count, :].rearrange("p h (q n) -> p (h q) n", n=LATENT),
            )

        def finish_round(r):
            scalar_relu(r, 1)
            store(r, 0, UNITS)

        for i in range(ROUNDS):
            if i >= 1:
                quantise_bank(i - 1, BANKS - 1)
            if i == 3:
                add_round(0)
            if i >= 3:
                add_round(i - 2)
            for b in range(BANKS):
                flip_bank(i, b)
                if b < BANKS - 1:
                    quantise_bank(i, b)
            if i == 0:
                quantise_global()
            if i == 2:
                compose_variants()
                global_and_bias()
                multiply_round(0)
            if i >= 2:
                multiply_round(i - 1)
            if i == 3:
                finish_round(0)
            if i >= 3:
                finish_round(i - 2)

        add_bank(ROUNDS - 2, 0)
        quantise_bank(ROUNDS - 1, BANKS - 1)
        multiply_round(ROUNDS - 1)
        scalar_relu(ROUNDS - 2, 0)
        add_bank(ROUNDS - 2, 1)
        scalar_relu(ROUNDS - 2, 1)
        store(ROUNDS - 2, 0, UNITS)
        for h in range(UNITS):
            add_bank(ROUNDS - 1, h)
            scalar_relu(ROUNDS - 1, h)
            store(ROUNDS - 1, h, 1)
